import numpy as np
import ml_dtypes


def mxq(x, axis, fmt="e4m3"):
    dtype, down = {"e4m3": (ml_dtypes.float8_e4m3fn, 7), "e5m2": (ml_dtypes.float8_e5m2, 14)}[fmt]
    v = np.moveaxis(np.asarray(x, np.float32).astype(ml_dtypes.bfloat16).astype(np.float64), axis, -1)
    blocks = v.reshape(v.shape[:-1] + (-1, 32))
    amax = np.abs(blocks).max(-1, keepdims=True)
    byte = np.maximum(np.where(amax > 0, np.frexp(amax)[1] - 1 + 127, 0) - down, 1)
    scale = np.exp2(byte - 127.0)
    codes = (blocks / scale).astype(np.float32).astype(dtype).astype(np.float64)
    return np.moveaxis((codes * scale).reshape(v.shape), -1, axis)


WIDE = False


def mx_kscale(k):
    if not WIDE:
        return np.ones(k)
    levels = np.array([20, -20, 10, -10, 0])
    a = np.random.permutation(np.resize(levels, k // 512 * 4)).reshape(k // 512, 4)
    idx = np.arange(k)
    return np.exp2(a[idx // 512, idx % 128 // 32])


BF16 = ml_dtypes.bfloat16


def bf(x):
    return np.asarray(x, np.float32).astype(BF16)


def f64(x):
    return np.asarray(x).astype(np.float64)


B, C, H, W, O, KH, KW = 8, 256, 32, 32, 128, 2, 2
STRIDE = (1, 1)
PAD = (1, 1)
DIL = (1, 1)
HO = H + 2 * PAD[0] - (KH - 1)
WO = W + 2 * PAD[1] - (KW - 1)
KG = KH * KW * O


def _grad_patches(g):
    b, o = g.shape[0], g.shape[1]
    rows = []
    for i in range(KH):
        for j in range(KW):
            r0 = PAD[0] - i
            c0 = PAD[1] - j
            rows.append(g[:, :, r0:r0 + H, c0:c0 + W])
    p = np.stack(rows, axis=1)
    p = p.reshape(b, KH * KW * o, H * W)
    return np.ascontiguousarray(np.swapaxes(p, 1, 2)).reshape(b * H * W, KH * KW * o)


def setup_inputs():
    u = mx_kscale(KG)[:O]
    x = np.random.standard_normal((B, C, H, W))
    weight = np.random.standard_normal((O, C, KH, KW)) / np.sqrt(C * KH * KW) / u[:, None, None, None]
    bias = np.random.standard_normal(O) * 0.5
    g = (np.random.standard_normal((B, O, HO, WO)) * np.exp2(np.random.randint(-12, 1, (B, 1, HO, WO)))
         * 8.0 * u[None, :, None, None])
    return {"x": bf(x), "weight": bf(weight), "bias": bf(bias), "grad_out": bf(g)}


def reference(x, weight, bias, grad_out):
    weight, g = f64(weight), f64(grad_out)
    b = g.shape[0]
    c = weight.shape[1]
    p = _grad_patches(g)
    wk = np.ascontiguousarray(weight.transpose(1, 2, 3, 0)).reshape(c, -1)
    gx = mxq(p, 1, "e5m2") @ mxq(wk, 1, "e4m3").T
    gx = gx.reshape(b, H * W, c)
    return np.ascontiguousarray(np.swapaxes(gx, 1, 2)).reshape(b, c, H, W)

@@ -1,0 +1,164 @@
+from contextlib import ExitStack
+
+import concourse.mybir as mybir
+
+BF16 = mybir.dt.bfloat16
+F32 = mybir.dt.float32
+I32 = mybir.dt.int32
+U32 = mybir.dt.uint32
+U8 = mybir.dt.uint8
+E4M3_X4 = mybir.dt.float8_e4m3fn_x4
+E5M2_X4 = mybir.dt.float8_e5m2_x4
+
+P = 128
+IMAGES, CHANNELS_OUT, GRAD_ROWS, GRAD_COLS = 8, 128, 33, 33
+CHANNELS_IN, ROWS, COLS = 256, 32, 32
+PACK = 4
+CHANNEL_PAIR = 2
+TAPS = 2
+SIDES = 2
+SIDE_PARTITIONS = P // SIDES
+IMAGE_PAIRS = IMAGES // SIDES
+C_HALVES = CHANNELS_IN // P
+BANDS = 2
+BAND_ROWS = ROWS // BANDS
+BAND_PIXELS = BAND_ROWS * COLS
+BAND_GRAD_ROWS = BAND_ROWS + 1
+BAND_WORDS = BAND_GRAD_ROWS * COLS
+HALF_COLS = COLS // 2
+UNITS = IMAGE_PAIRS * BANDS
+SCALE_PITCH = 576
+
+FLOPS = 2 * IMAGES * ROWS * COLS * TAPS * TAPS * CHANNELS_OUT * CHANNELS_IN
+BYTES = (
+    2 * CHANNELS_OUT * CHANNELS_IN * TAPS * TAPS
+    + 2 * IMAGES * CHANNELS_OUT * GRAD_ROWS * GRAD_COLS
+    + 4 * IMAGES * CHANNELS_IN * ROWS * COLS
+)
+
+
+def tile_customconvmodule_t_kernel(tc, x, weight, bias, grad_out, out):
+    nc = tc.nc
+    with ExitStack() as ctx:
+        keep = ctx.enter_context(tc.tile_pool(name="keep", bufs=1))
+        raw_pool = ctx.enter_context(tc.tile_pool(name="raw", bufs=UNITS))
+        grouped_pool = ctx.enter_context(tc.tile_pool(name="grouped", bufs=3))
+        result_pool = ctx.enter_context(tc.tile_pool(name="result", bufs=6))
+        psum = ctx.enter_context(tc.psum_pool(name="psum", bufs=8))
+
+        grad_codes = keep.tile([P, UNITS, BAND_WORDS], U32, align_bytes=64)
+        grad_scales = keep.tile([P, UNITS, SCALE_PITCH], U8, align_bytes=64)
+        grad_scales_down = keep.tile([P, UNITS, BAND_PIXELS], U8, align_bytes=64)
+        nc.vector.memset(grad_scales[:].bitcast(I32), 0)
+
+        grad_rows = grad_out.rearrange("b (q e) r s -> (b q) e r s", e=CHANNEL_PAIR)
+        raws = []
+        for pair in range(IMAGE_PAIRS):
+            for band in range(BANDS):
+                raw = raw_pool.tile([P, CHANNEL_PAIR, BAND_GRAD_ROWS, GRAD_COLS], BF16)
+                first_row = band * BAND_ROWS
+                nc.sync.dma_start(
+                    out=raw[:],
+                    in_=grad_rows[
+                        pair * P : (pair + 1) * P, :, first_row : first_row + BAND_GRAD_ROWS, :
+                    ],
+                )
+                raws.append(raw)
+
+        weight_rows = weight.rearrange("(q e) c i j -> q (e c i j)", e=CHANNEL_PAIR)
+        weight_raw = keep.tile([P, CHANNEL_PAIR, CHANNELS_IN, TAPS, TAPS], BF16)
+        for side in range(SIDES):
+            side_rows = slice(side * SIDE_PARTITIONS, (side + 1) * SIDE_PARTITIONS)
+            nc.scalar.dma_start(
+                out=weight_raw[side_rows].rearrange("q e c i j -> q (e c i j)"), in_=weight_rows
+            )
+
+        weight_grouped = keep.tile(
+            [P, TAPS, CHANNELS_IN, CHANNEL_PAIR, TAPS], BF16, align_bytes=64
+        )
+        for right in range(TAPS):
+            nc.vector.tensor_copy(
+                out=weight_grouped[:, :, :, :, right],
+                in_=weight_raw[:, :, :, :, 1 - right].rearrange("q e c i -> q i c e"),
+            )
+        weight_codes = keep.tile([P, TAPS * CHANNELS_IN], U32, align_bytes=64)
+        weight_scales = keep.tile([P, TAPS * CHANNELS_IN], U8, align_bytes=64)
+        nc.vector.quantize_mx(
+            out=weight_codes[:].bitcast(E4M3_X4),
+            scales=weight_scales[:],
+            in_=weight_grouped[:].rearrange("q i c e j -> q (i c e j)"),
+        )
+        side_codes = keep.tile([P, SIDES, TAPS * CHANNELS_IN], U32, align_bytes=64)
+        nc.vector.memset(side_codes[:].bitcast(I32), 0)
+        for side in range(SIDES):
+            side_rows = slice(side * SIDE_PARTITIONS, (side + 1) * SIDE_PARTITIONS)
+            nc.vector.tensor_copy(
+                out=side_codes[side_rows, side, :].bitcast(I32),
+                in_=weight_codes[side_rows, :].bitcast(I32),
+            )
+
+        for pair in range(IMAGE_PAIRS):
+            for band in range(BANDS):
+                unit = pair * BANDS + band
+                raw = raws[unit]
+
+                grouped = grouped_pool.tile(
+                    [P, BAND_GRAD_ROWS, 2, HALF_COLS, CHANNEL_PAIR, TAPS], BF16, align_bytes=64
+                )
+                for parity in range(2):
+                    nc.vector.tensor_copy(
+                        out=grouped[:, :, parity, :, :, :],
+                        in_=raw[:, :, :, parity : parity + COLS].rearrange(
+                            "q e r (v j) -> q r v e j", j=TAPS
+                        ),
+                    )
+
+                values = grouped[:].rearrange("q r y v e j -> q (r y v e j)")
+                for first_word, end_word in ((0, BAND_PIXELS), (BAND_PIXELS, BAND_WORDS)):
+                    nc.vector.quantize_mx(
+                        out=grad_codes[:, unit, first_word:end_word].bitcast(E5M2_X4),
+                        scales=grad_scales[:, unit, first_word:end_word],
+                        in_=values[:, first_word * PACK : end_word * PACK],
+                    )
+                nc.vector.tensor_copy(
+                    out=grad_scales_down[:, unit, :].bitcast(I32),
+                    in_=grad_scales[:, unit, COLS:BAND_WORDS].bitcast(I32),
+                )
+
+                for side in range(SIDES):
+                    result = result_pool.tile([P, C_HALVES, BAND_PIXELS], F32)
+                    for half in range(C_HALVES):
+                        acc = psum.tile([P, BAND_PIXELS], F32)
+                        for down in range(TAPS):
+                            c_words = slice(
+                                (1 - down) * CHANNELS_IN + half * P,
+                                (1 - down) * CHANNELS_IN + (half + 1) * P,
+                            )
+                            nc.tensor.matmul_mx(
+                                out=acc[:],
+                                lhsT=side_codes[:, side, c_words].bitcast(E4M3_X4),
+                                lhsT_scale=weight_scales[:, c_words],
+                                rhs=grad_codes[
+                                    :, unit, down * COLS : down * COLS + BAND_PIXELS
+                                ].bitcast(E5M2_X4),
+                                rhs_scale=(
+                                    grad_scales[:, unit, 0:BAND_PIXELS]
+                                    if down == 0
+                                    else grad_scales_down[:, unit, :]
+                                ),
+                                start=(down == 0),
+                                stop=(down == TAPS - 1),
+                            )
+                        nc.scalar.copy(
+                            out=result[:, half, :].rearrange(
+                                "c (r v y) -> c r v y", v=HALF_COLS, y=2
+                            ),
+                            in_=acc[:].rearrange("c (r y v) -> c r v y", y=2, v=HALF_COLS),
+                        )
+                    image = pair * SIDES + side
+                    nc.sync.dma_start(
+                        out=out[image].rearrange("(half c) h w -> c half (h w)", half=C_HALVES)[
+                            :, :, band * BAND_PIXELS : (band + 1) * BAND_PIXELS
+                        ],
+                        in_=result[:],
+                    )

@@ -43,14 +43,30 @@ def tile_customconvmodule_t_kernel(tc, x, weight, bias, grad_out, out):
         keep = ctx.enter_context(tc.tile_pool(name="keep", bufs=1))
         raw_pool = ctx.enter_context(tc.tile_pool(name="raw", bufs=UNITS))
         grouped_pool = ctx.enter_context(tc.tile_pool(name="grouped", bufs=3))
-        result_pool = ctx.enter_context(tc.tile_pool(name="result", bufs=6))
+        result_pool = ctx.enter_context(tc.tile_pool(name="result", bufs=8))
         psum = ctx.enter_context(tc.psum_pool(name="psum", bufs=8))
+        ctx.enter_context(tc.manual_schedule())
 
         grad_codes = keep.tile([P, UNITS, BAND_WORDS], U32, align_bytes=64)
         grad_scales = keep.tile([P, UNITS, SCALE_PITCH], U8, align_bytes=64)
         grad_scales_down = keep.tile([P, UNITS, BAND_PIXELS], U8, align_bytes=64)
-        nc.vector.memset(grad_scales[:].bitcast(I32), 0)
+        weight_raw = keep.tile([P, CHANNEL_PAIR, CHANNELS_IN, TAPS, TAPS], BF16)
+        weight_grouped = keep.tile(
+            [P, TAPS, CHANNELS_IN, CHANNEL_PAIR, TAPS], BF16, align_bytes=64
+        )
+        weight_codes = keep.tile([P, TAPS * CHANNELS_IN], U32, align_bytes=64)
+        weight_scales = keep.tile([P, TAPS * CHANNELS_IN], U8, align_bytes=64)
+        side_codes = keep.tile([P, SIDES, TAPS * CHANNELS_IN], U32, align_bytes=64)
 
+        nc.vector.memset(grad_scales[:].bitcast(I32), 0)
+        nc.vector.memset(side_codes[:].bitcast(I32), 0)
+
+        weight_rows = weight.rearrange("(q e) c i j -> q (e c i j)", e=CHANNEL_PAIR)
+        for side in range(SIDES):
+            side_rows = slice(side * SIDE_PARTITIONS, (side + 1) * SIDE_PARTITIONS)
+            nc.sync.dma_start(
+                out=weight_raw[side_rows].rearrange("q e c i j -> q (e c i j)"), in_=weight_rows
+            )
         grad_rows = grad_out.rearrange("b (q e) r s -> (b q) e r s", e=CHANNEL_PAIR)
         raws = []
         for pair in range(IMAGE_PAIRS):
@@ -65,100 +81,107 @@ def tile_customconvmodule_t_kernel(tc, x, weight, bias, grad_out, out):
                 )
                 raws.append(raw)
 
-        weight_rows = weight.rearrange("(q e) c i j -> q (e c i j)", e=CHANNEL_PAIR)
-        weight_raw = keep.tile([P, CHANNEL_PAIR, CHANNELS_IN, TAPS, TAPS], BF16)
-        for side in range(SIDES):
-            side_rows = slice(side * SIDE_PARTITIONS, (side + 1) * SIDE_PARTITIONS)
-            nc.scalar.dma_start(
-                out=weight_raw[side_rows].rearrange("q e c i j -> q (e c i j)"), in_=weight_rows
+        def group_weight():
+            for right in range(TAPS):
+                nc.scalar.copy(
+                    out=weight_grouped[:, :, :, :, right],
+                    in_=weight_raw[:, :, :, :, 1 - right].rearrange("q e c i -> q i c e"),
+                )
+
+        def quantise_weight():
+            nc.vector.quantize_mx(
+                out=weight_codes[:].bitcast(E4M3_X4),
+                scales=weight_scales[:],
+                in_=weight_grouped[:].rearrange("q i c e j -> q (i c e j)"),
             )
 
-        weight_grouped = keep.tile(
-            [P, TAPS, CHANNELS_IN, CHANNEL_PAIR, TAPS], BF16, align_bytes=64
-        )
-        for right in range(TAPS):
-            nc.vector.tensor_copy(
-                out=weight_grouped[:, :, :, :, right],
-                in_=weight_raw[:, :, :, :, 1 - right].rearrange("q e c i -> q i c e"),
-            )
-        weight_codes = keep.tile([P, TAPS * CHANNELS_IN], U32, align_bytes=64)
-        weight_scales = keep.tile([P, TAPS * CHANNELS_IN], U8, align_bytes=64)
-        nc.vector.quantize_mx(
-            out=weight_codes[:].bitcast(E4M3_X4),
-            scales=weight_scales[:],
-            in_=weight_grouped[:].rearrange("q i c e j -> q (i c e j)"),
-        )
-        side_codes = keep.tile([P, SIDES, TAPS * CHANNELS_IN], U32, align_bytes=64)
-        nc.vector.memset(side_codes[:].bitcast(I32), 0)
-        for side in range(SIDES):
-            side_rows = slice(side * SIDE_PARTITIONS, (side + 1) * SIDE_PARTITIONS)
-            nc.vector.tensor_copy(
-                out=side_codes[side_rows, side, :].bitcast(I32),
-                in_=weight_codes[side_rows, :].bitcast(I32),
-            )
+        def copy_weight_to_sides():
+            for side in range(SIDES):
+                side_rows = slice(side * SIDE_PARTITIONS, (side + 1) * SIDE_PARTITIONS)
+                nc.vector.tensor_copy(
+                    out=side_codes[side_rows, side, :].bitcast(I32),
+                    in_=weight_codes[side_rows, :].bitcast(I32),
+                )
 
-        for pair in range(IMAGE_PAIRS):
-            for band in range(BANDS):
-                unit = pair * BANDS + band
-                raw = raws[unit]
+        groupeds = []
 
+        def group(unit, parity):
+            if parity == 0:
                 grouped = grouped_pool.tile(
                     [P, BAND_GRAD_ROWS, 2, HALF_COLS, CHANNEL_PAIR, TAPS], BF16, align_bytes=64
                 )
-                for parity in range(2):
-                    nc.vector.tensor_copy(
-                        out=grouped[:, :, parity, :, :, :],
-                        in_=raw[:, :, :, parity : parity + COLS].rearrange(
-                            "q e r (v j) -> q r v e j", j=TAPS
-                        ),
-                    )
+                groupeds.append(grouped)
+            nc.vector.tensor_copy(
+                out=groupeds[unit][:, :, parity, :, :, :],
+                in_=raws[unit][:, :, :, parity : parity + COLS].rearrange(
+                    "q e r (v j) -> q r v e j", j=TAPS
+                ),
+            )
 
-                values = grouped[:].rearrange("q r y v e j -> q (r y v e j)")
-                for first_word, end_word in ((0, BAND_PIXELS), (BAND_PIXELS, BAND_WORDS)):
-                    nc.vector.quantize_mx(
-                        out=grad_codes[:, unit, first_word:end_word].bitcast(E5M2_X4),
-                        scales=grad_scales[:, unit, first_word:end_word],
-                        in_=values[:, first_word * PACK : end_word * PACK],
-                    )
-                nc.vector.tensor_copy(
-                    out=grad_scales_down[:, unit, :].bitcast(I32),
-                    in_=grad_scales[:, unit, COLS:BAND_WORDS].bitcast(I32),
+        def quantise(unit):
+            values = groupeds[unit][:].rearrange("q r y v e j -> q (r y v e j)")
+            for first_word, end_word in ((0, BAND_PIXELS), (BAND_PIXELS, BAND_WORDS)):
+                nc.vector.quantize_mx(
+                    out=grad_codes[:, unit, first_word:end_word].bitcast(E5M2_X4),
+                    scales=grad_scales[:, unit, first_word:end_word],
+                    in_=values[:, first_word * PACK : end_word * PACK],
                 )
 
-                for side in range(SIDES):
-                    result = result_pool.tile([P, C_HALVES, BAND_PIXELS], F32)
-                    for half in range(C_HALVES):
-                        acc = psum.tile([P, BAND_PIXELS], F32)
-                        for down in range(TAPS):
-                            c_words = slice(
-                                (1 - down) * CHANNELS_IN + half * P,
-                                (1 - down) * CHANNELS_IN + (half + 1) * P,
-                            )
-                            nc.tensor.matmul_mx(
-                                out=acc[:],
-                                lhsT=side_codes[:, side, c_words].bitcast(E4M3_X4),
-                                lhsT_scale=weight_scales[:, c_words],
-                                rhs=grad_codes[
-                                    :, unit, down * COLS : down * COLS + BAND_PIXELS
-                                ].bitcast(E5M2_X4),
-                                rhs_scale=(
-                                    grad_scales[:, unit, 0:BAND_PIXELS]
-                                    if down == 0
-                                    else grad_scales_down[:, unit, :]
-                                ),
-                                start=(down == 0),
-                                stop=(down == TAPS - 1),
-                            )
-                        nc.scalar.copy(
-                            out=result[:, half, :].rearrange(
-                                "c (r v y) -> c r v y", v=HALF_COLS, y=2
-                            ),
-                            in_=acc[:].rearrange("c (r y v) -> c r v y", y=2, v=HALF_COLS),
+        def shift_scales(unit):
+            nc.vector.tensor_copy(
+                out=grad_scales_down[:, unit, :].bitcast(I32),
+                in_=grad_scales[:, unit, COLS:BAND_WORDS].bitcast(I32),
+            )
+
+        def multiply_and_store(unit):
+            pair, band = divmod(unit, BANDS)
+            for side in range(SIDES):
+                result = result_pool.tile([P, C_HALVES, BAND_PIXELS], F32)
+                for half in range(C_HALVES):
+                    acc = psum.tile([P, BAND_PIXELS], F32)
+                    for down in range(TAPS):
+                        c_words = slice(
+                            (1 - down) * CHANNELS_IN + half * P,
+                            (1 - down) * CHANNELS_IN + (half + 1) * P,
                         )
-                    image = pair * SIDES + side
-                    nc.sync.dma_start(
-                        out=out[image].rearrange("(half c) h w -> c half (h w)", half=C_HALVES)[
-                            :, :, band * BAND_PIXELS : (band + 1) * BAND_PIXELS
-                        ],
-                        in_=result[:],
+                        nc.tensor.matmul_mx(
+                            out=acc[:],
+                            lhsT=side_codes[:, side, c_words].bitcast(E4M3_X4),
+                            lhsT_scale=weight_scales[:, c_words],
+                            rhs=grad_codes[
+                                :, unit, down * COLS : down * COLS + BAND_PIXELS
+                            ].bitcast(E5M2_X4),
+                            rhs_scale=(
+                                grad_scales[:, unit, 0:BAND_PIXELS]
+                                if down == 0
+                                else grad_scales_down[:, unit, :]
+                            ),
+                            start=(down == 0),
+                            stop=(down == TAPS - 1),
+                        )
+                    nc.scalar.copy(
+                        out=result[:, half, :].rearrange("c (r v y) -> c r v y", v=HALF_COLS, y=2),
+                        in_=acc[:].rearrange("c (r y v) -> c r v y", y=2, v=HALF_COLS),
                     )
+                nc.sync.dma_start(
+                    out=out[pair * SIDES + side].rearrange(
+                        "(half c) h w -> c half (h w)", half=C_HALVES
+                    )[:, :, band * BAND_PIXELS : (band + 1) * BAND_PIXELS],
+                    in_=result[:],
+                )
+
+        group_weight()
+        group(0, 0)
+        group(0, 1)
+        for unit in range(UNITS):
+            if unit + 1 < UNITS:
+                group(unit + 1, 0)
+            quantise(unit)
+            if unit == 0:
+                quantise_weight()
+            if unit + 1 < UNITS:
+                group(unit + 1, 1)
+            shift_scales(unit)
+            if unit == 0:
+                copy_weight_to_sides()
+            multiply_and_store(unit)

@@ -111,12 +111,13 @@ def tile_customconvmodule_t_kernel(tc, x, weight, bias, grad_out, out):
                     [P, BAND_GRAD_ROWS, 2, HALF_COLS, CHANNEL_PAIR, TAPS], BF16, align_bytes=64
                 )
                 groupeds.append(grouped)
-            nc.vector.tensor_copy(
-                out=groupeds[unit][:, :, parity, :, :, :],
-                in_=raws[unit][:, :, :, parity : parity + COLS].rearrange(
-                    "q e r (v j) -> q r v e j", j=TAPS
-                ),
-            )
+            for first_row, end_row in ((0, BAND_ROWS), (BAND_ROWS, BAND_GRAD_ROWS)):
+                nc.vector.tensor_copy(
+                    out=groupeds[unit][:, first_row:end_row, parity, :, :, :],
+                    in_=raws[unit][:, :, first_row:end_row, parity : parity + COLS].rearrange(
+                        "q e r (v j) -> q r v e j", j=TAPS
+                    ),
+                )
 
         def quantise(unit):
             values = groupeds[unit][:].rearrange("q r y v e j -> q (r y v e j)")

@@ -58,15 +58,18 @@ def tile_customconvmodule_t_kernel(tc, x, weight, bias, grad_out, out):
         weight_scales = keep.tile([P, TAPS * CHANNELS_IN], U8, align_bytes=64)
         side_codes = keep.tile([P, SIDES, TAPS * CHANNELS_IN], U32, align_bytes=64)
 
-        nc.vector.memset(grad_scales[:].bitcast(I32), 0)
         nc.vector.memset(side_codes[:].bitcast(I32), 0)
+        nc.vector.memset(grad_scales[:].bitcast(I32), 0)
 
         weight_rows = weight.rearrange("(q e) c i j -> q (e c i j)", e=CHANNEL_PAIR)
         for side in range(SIDES):
             side_rows = slice(side * SIDE_PARTITIONS, (side + 1) * SIDE_PARTITIONS)
-            nc.sync.dma_start(
+            nc.scalar.dma_start(
                 out=weight_raw[side_rows].rearrange("q e c i j -> q (e c i j)"), in_=weight_rows
             )
+        table_warmer = keep.tile([P, 2], F32)
+        nc.gpsimd.memset(table_warmer[:, 0:1], 0.0)
+        nc.scalar.copy(out=table_warmer[:, 1:2], in_=table_warmer[:, 0:1])
         grad_rows = grad_out.rearrange("b (q e) r s -> (b q) e r s", e=CHANNEL_PAIR)
         raws = []
         for pair in range(IMAGE_PAIRS):
@@ -81,26 +84,27 @@ def tile_customconvmodule_t_kernel(tc, x, weight, bias, grad_out, out):
                 )
                 raws.append(raw)
 
-        def group_weight():
-            for right in range(TAPS):
-                nc.scalar.copy(
-                    out=weight_grouped[:, :, :, :, right],
-                    in_=weight_raw[:, :, :, :, 1 - right].rearrange("q e c i -> q i c e"),
-                )
-
-        def quantise_weight():
-            nc.vector.quantize_mx(
-                out=weight_codes[:].bitcast(E4M3_X4),
-                scales=weight_scales[:],
-                in_=weight_grouped[:].rearrange("q i c e j -> q (i c e j)"),
+        def group_weight(i):
+            nc.scalar.copy(
+                out=weight_grouped[:, i, :, :, :],
+                in_=weight_raw[:, :, :, i, ::-1].rearrange("q e c j -> q c e j"),
             )
 
-        def copy_weight_to_sides():
+        def quantise_weight(i):
+            i_words = slice(i * CHANNELS_IN, (i + 1) * CHANNELS_IN)
+            nc.vector.quantize_mx(
+                out=weight_codes[:, i_words].bitcast(E4M3_X4),
+                scales=weight_scales[:, i_words],
+                in_=weight_grouped[:, i, :, :, :].rearrange("q c e j -> q (c e j)"),
+            )
+
+        def copy_weight_to_sides(i):
+            i_words = slice(i * CHANNELS_IN, (i + 1) * CHANNELS_IN)
             for side in range(SIDES):
                 side_rows = slice(side * SIDE_PARTITIONS, (side + 1) * SIDE_PARTITIONS)
                 nc.vector.tensor_copy(
-                    out=side_codes[side_rows, side, :].bitcast(I32),
-                    in_=weight_codes[side_rows, :].bitcast(I32),
+                    out=side_codes[side_rows, side, i_words].bitcast(I32),
+                    in_=weight_codes[side_rows, i_words].bitcast(I32),
                 )
 
         groupeds = []
@@ -119,9 +123,10 @@ def tile_customconvmodule_t_kernel(tc, x, weight, bias, grad_out, out):
                     ),
                 )
 
-        def quantise(unit):
+        def quantise(unit, parts=(0, 1)):
             values = groupeds[unit][:].rearrange("q r y v e j -> q (r y v e j)")
-            for first_word, end_word in ((0, BAND_PIXELS), (BAND_PIXELS, BAND_WORDS)):
+            for part in parts:
+                first_word, end_word = ((0, BAND_PIXELS), (BAND_PIXELS, BAND_WORDS))[part]
                 nc.vector.quantize_mx(
                     out=grad_codes[:, unit, first_word:end_word].bitcast(E5M2_X4),
                     scales=grad_scales[:, unit, first_word:end_word],
@@ -134,55 +139,80 @@ def tile_customconvmodule_t_kernel(tc, x, weight, bias, grad_out, out):
                 in_=grad_scales[:, unit, COLS:BAND_WORDS].bitcast(I32),
             )
 
-        def multiply_and_store(unit):
+        def one_pass(unit, side, half, down, acc):
+            c_words = slice(
+                (1 - down) * CHANNELS_IN + half * P, (1 - down) * CHANNELS_IN + (half + 1) * P
+            )
+            nc.tensor.matmul_mx(
+                out=acc[:],
+                lhsT=side_codes[:, side, c_words].bitcast(E4M3_X4),
+                lhsT_scale=weight_scales[:, c_words],
+                rhs=grad_codes[:, unit, down * COLS : down * COLS + BAND_PIXELS].bitcast(E5M2_X4),
+                rhs_scale=(
+                    grad_scales[:, unit, 0:BAND_PIXELS]
+                    if down == 0
+                    else grad_scales_down[:, unit, :]
+                ),
+                start=(down == 0),
+                stop=(down == TAPS - 1),
+            )
+
+        def empty_and_store(unit, side, accs):
             pair, band = divmod(unit, BANDS)
+            result = result_pool.tile([P, C_HALVES, BAND_PIXELS], F32)
+            for half in range(C_HALVES):
+                nc.scalar.copy(
+                    out=result[:, half, :].rearrange("c (r v y) -> c r v y", v=HALF_COLS, y=2),
+                    in_=accs[half][:].rearrange("c (r y v) -> c r v y", y=2, v=HALF_COLS),
+                )
+            nc.sync.dma_start(
+                out=out[pair * SIDES + side].rearrange(
+                    "(half c) h w -> c half (h w)", half=C_HALVES
+                )[:, :, band * BAND_PIXELS : (band + 1) * BAND_PIXELS],
+                in_=result[:],
+            )
+
+        def multiply_and_store(unit):
             for side in range(SIDES):
-                result = result_pool.tile([P, C_HALVES, BAND_PIXELS], F32)
+                accs = []
                 for half in range(C_HALVES):
                     acc = psum.tile([P, BAND_PIXELS], F32)
+                    accs.append(acc)
                     for down in range(TAPS):
-                        c_words = slice(
-                            (1 - down) * CHANNELS_IN + half * P,
-                            (1 - down) * CHANNELS_IN + (half + 1) * P,
-                        )
-                        nc.tensor.matmul_mx(
-                            out=acc[:],
-                            lhsT=side_codes[:, side, c_words].bitcast(E4M3_X4),
-                            lhsT_scale=weight_scales[:, c_words],
-                            rhs=grad_codes[
-                                :, unit, down * COLS : down * COLS + BAND_PIXELS
-                            ].bitcast(E5M2_X4),
-                            rhs_scale=(
-                                grad_scales[:, unit, 0:BAND_PIXELS]
-                                if down == 0
-                                else grad_scales_down[:, unit, :]
-                            ),
-                            start=(down == 0),
-                            stop=(down == TAPS - 1),
-                        )
-                    nc.scalar.copy(
-                        out=result[:, half, :].rearrange("c (r v y) -> c r v y", v=HALF_COLS, y=2),
-                        in_=acc[:].rearrange("c (r y v) -> c r v y", y=2, v=HALF_COLS),
-                    )
-                nc.sync.dma_start(
-                    out=out[pair * SIDES + side].rearrange(
-                        "(half c) h w -> c half (h w)", half=C_HALVES
-                    )[:, :, band * BAND_PIXELS : (band + 1) * BAND_PIXELS],
-                    in_=result[:],
-                )
+                        one_pass(unit, side, half, down, acc)
+                empty_and_store(unit, side, accs)
 
-        group_weight()
+        def multiply_and_store_first(unit):
+            accs = []
+            for bank in range(SIDES * C_HALVES):
+                acc = psum.tile([P, BAND_PIXELS], F32)
+                accs.append(acc)
+            for down in range(TAPS):
+                for side in range(SIDES):
+                    for half in range(C_HALVES):
+                        one_pass(unit, side, half, down, accs[side * C_HALVES + half])
+            for side in range(SIDES):
+                empty_and_store(unit, side, accs[side * C_HALVES : (side + 1) * C_HALVES])
+
+        group_weight(1)
+        group_weight(0)
         group(0, 0)
         group(0, 1)
-        for unit in range(UNITS):
+        quantise(0, (0,))
+        quantise_weight(1)
+        quantise(0, (1,))
+        copy_weight_to_sides(1)
+        shift_scales(0)
+        quantise_weight(0)
+        group(1, 0)
+        copy_weight_to_sides(0)
+        group(1, 1)
+        multiply_and_store_first(0)
+        for unit in range(1, UNITS):
             if unit + 1 < UNITS:
                 group(unit + 1, 0)
             quantise(unit)
-            if unit == 0:
-                quantise_weight()
             if unit + 1 < UNITS:
                 group(unit + 1, 1)
             shift_scales(unit)
-            if unit == 0:
-                copy_weight_to_sides()
             multiply_and_store(unit)

@@ -28,6 +28,8 @@ BAND_WORDS = BAND_GRAD_ROWS * COLS
 HALF_COLS = COLS // 2
 UNITS = IMAGE_PAIRS * BANDS
 SCALE_PITCH = 576
+BAND_VALUES = BAND_GRAD_ROWS * GRAD_COLS
+PLANE_PITCH = 576
 
 FLOPS = 2 * IMAGES * ROWS * COLS * TAPS * TAPS * CHANNELS_OUT * CHANNELS_IN
 BYTES = (
@@ -74,15 +76,15 @@ def tile_customconvmodule_t_kernel(tc, x, weight, bias, grad_out, out):
         raws = []
         for pair in range(IMAGE_PAIRS):
             for band in range(BANDS):
-                raw = raw_pool.tile([P, CHANNEL_PAIR, BAND_GRAD_ROWS, GRAD_COLS], BF16)
+                raw = raw_pool.tile([P, CHANNEL_PAIR, PLANE_PITCH], BF16, align_bytes=64)
                 first_row = band * BAND_ROWS
                 nc.sync.dma_start(
-                    out=raw[:],
+                    out=raw[:, :, 0:BAND_VALUES],
                     in_=grad_rows[
                         pair * P : (pair + 1) * P, :, first_row : first_row + BAND_GRAD_ROWS, :
-                    ],
+                    ].rearrange("p e r s -> p e (r s)"),
                 )
-                raws.append(raw)
+                raws.append(raw[:, :, 0:BAND_VALUES].rearrange("p e (r s) -> p e r s", s=GRAD_COLS))
 
         def group_weight(i):
             nc.scalar.copy(

@@ -29,6 +29,7 @@ HALF_COLS = COLS // 2
 UNITS = IMAGE_PAIRS * BANDS
 SCALE_PITCH = 576
 BAND_VALUES = BAND_GRAD_ROWS * GRAD_COLS
+HALF_WORDS = TAPS * P
 PLANE_PITCH = 576
 
 FLOPS = 2 * IMAGES * ROWS * COLS * TAPS * TAPS * CHANNELS_OUT * CHANNELS_IN
@@ -54,7 +55,7 @@ def tile_customconvmodule_t_kernel(tc, x, weight, bias, grad_out, out):
         grad_scales_down = keep.tile([P, UNITS, BAND_PIXELS], U8, align_bytes=64)
         weight_raw = keep.tile([P, CHANNEL_PAIR, CHANNELS_IN, TAPS, TAPS], BF16)
         weight_grouped = keep.tile(
-            [P, TAPS, CHANNELS_IN, CHANNEL_PAIR, TAPS], BF16, align_bytes=64
+            [P, C_HALVES, TAPS, P, CHANNEL_PAIR, TAPS], BF16, align_bytes=64
         )
         weight_codes = keep.tile([P, TAPS * CHANNELS_IN], U32, align_bytes=64)
         weight_scales = keep.tile([P, TAPS * CHANNELS_IN], U8, align_bytes=64)
@@ -86,27 +87,29 @@ def tile_customconvmodule_t_kernel(tc, x, weight, bias, grad_out, out):
                 )
                 raws.append(raw[:, :, 0:BAND_VALUES].rearrange("p e (r s) -> p e r s", s=GRAD_COLS))
 
-        def group_weight(i):
+        def group_weight(half):
             nc.scalar.copy(
-                out=weight_grouped[:, i, :, :, :],
-                in_=weight_raw[:, :, :, i, ::-1].rearrange("q e c j -> q c e j"),
+                out=weight_grouped[:, half, :, :, :, :],
+                in_=weight_raw[:, :, half * P : (half + 1) * P, :, ::-1].rearrange(
+                    "q e c i j -> q i c e j"
+                ),
             )
 
-        def quantise_weight(i):
-            i_words = slice(i * CHANNELS_IN, (i + 1) * CHANNELS_IN)
+        def quantise_weight(half):
+            half_words = slice(half * HALF_WORDS, (half + 1) * HALF_WORDS)
             nc.vector.quantize_mx(
-                out=weight_codes[:, i_words].bitcast(E4M3_X4),
-                scales=weight_scales[:, i_words],
-                in_=weight_grouped[:, i, :, :, :].rearrange("q c e j -> q (c e j)"),
+                out=weight_codes[:, half_words].bitcast(E4M3_X4),
+                scales=weight_scales[:, half_words],
+                in_=weight_grouped[:, half, :, :, :, :].rearrange("q i c e j -> q (i c e j)"),
             )
 
-        def copy_weight_to_sides(i):
-            i_words = slice(i * CHANNELS_IN, (i + 1) * CHANNELS_IN)
+        def copy_weight_to_sides(half):
+            half_words = slice(half * HALF_WORDS, (half + 1) * HALF_WORDS)
             for side in range(SIDES):
                 side_rows = slice(side * SIDE_PARTITIONS, (side + 1) * SIDE_PARTITIONS)
                 nc.vector.tensor_copy(
-                    out=side_codes[side_rows, side, i_words].bitcast(I32),
-                    in_=weight_codes[side_rows, i_words].bitcast(I32),
+                    out=side_codes[side_rows, side, half_words].bitcast(I32),
+                    in_=weight_codes[side_rows, half_words].bitcast(I32),
                 )
 
         groupeds = []
@@ -142,9 +145,8 @@ def tile_customconvmodule_t_kernel(tc, x, weight, bias, grad_out, out):
             )
 
         def one_pass(unit, side, half, down, acc):
-            c_words = slice(
-                (1 - down) * CHANNELS_IN + half * P, (1 - down) * CHANNELS_IN + (half + 1) * P
-            )
+            first_c_word = half * HALF_WORDS + (1 - down) * P
+            c_words = slice(first_c_word, first_c_word + P)
             nc.tensor.matmul_mx(
                 out=acc[:],
                 lhsT=side_codes[:, side, c_words].bitcast(E4M3_X4),
@@ -185,29 +187,36 @@ def tile_customconvmodule_t_kernel(tc, x, weight, bias, grad_out, out):
                 empty_and_store(unit, side, accs)
 
         def multiply_and_store_first(unit):
-            accs = []
-            for bank in range(SIDES * C_HALVES):
-                acc = psum.tile([P, BAND_PIXELS], F32)
-                accs.append(acc)
-            for down in range(TAPS):
+            pair, band = divmod(unit, BANDS)
+            for half in range(C_HALVES):
                 for side in range(SIDES):
-                    for half in range(C_HALVES):
-                        one_pass(unit, side, half, down, accs[side * C_HALVES + half])
-            for side in range(SIDES):
-                empty_and_store(unit, side, accs[side * C_HALVES : (side + 1) * C_HALVES])
+                    acc = psum.tile([P, BAND_PIXELS], F32)
+                    for down in range(TAPS):
+                        one_pass(unit, side, half, down, acc)
+                    bank_result = result_pool.tile([P, BAND_PIXELS], F32)
+                    nc.scalar.copy(
+                        out=bank_result[:].rearrange("c (r v y) -> c r v y", v=HALF_COLS, y=2),
+                        in_=acc[:].rearrange("c (r y v) -> c r v y", y=2, v=HALF_COLS),
+                    )
+                    nc.sync.dma_start(
+                        out=out[pair * SIDES + side, half * P : (half + 1) * P].rearrange(
+                            "c h w -> c (h w)"
+                        )[:, band * BAND_PIXELS : (band + 1) * BAND_PIXELS],
+                        in_=bank_result[:],
+                    )
 
-        group_weight(1)
         group_weight(0)
+        group_weight(1)
         group(0, 0)
         group(0, 1)
         quantise(0, (0,))
-        quantise_weight(1)
-        quantise(0, (1,))
-        copy_weight_to_sides(1)
-        shift_scales(0)
         quantise_weight(0)
-        group(1, 0)
+        quantise(0, (1,))
         copy_weight_to_sides(0)
+        shift_scales(0)
+        quantise_weight(1)
+        group(1, 0)
+        copy_weight_to_sides(1)
         group(1, 1)
         multiply_and_store_first(0)
         for unit in range(1, UNITS):

@@ -29,6 +29,7 @@ HALF_COLS = COLS // 2
 UNITS = IMAGE_PAIRS * BANDS
 SCALE_PITCH = 576
 BAND_VALUES = BAND_GRAD_ROWS * GRAD_COLS
+FIRST_SHARED_UNIT = 5
 HALF_WORDS = TAPS * P
 PLANE_PITCH = 576
 
@@ -161,30 +162,34 @@ def tile_customconvmodule_t_kernel(tc, x, weight, bias, grad_out, out):
                 stop=(down == TAPS - 1),
             )
 
-        def empty_and_store(unit, side, accs):
-            pair, band = divmod(unit, BANDS)
-            result = result_pool.tile([P, C_HALVES, BAND_PIXELS], F32)
-            for half in range(C_HALVES):
-                nc.scalar.copy(
-                    out=result[:, half, :].rearrange("c (r v y) -> c r v y", v=HALF_COLS, y=2),
-                    in_=accs[half][:].rearrange("c (r y v) -> c r v y", y=2, v=HALF_COLS),
-                )
-            nc.sync.dma_start(
-                out=out[pair * SIDES + side].rearrange(
-                    "(half c) h w -> c half (h w)", half=C_HALVES
-                )[:, :, band * BAND_PIXELS : (band + 1) * BAND_PIXELS],
-                in_=result[:],
+        def empty(copy, acc, target):
+            copy(
+                out=target.rearrange("c (r v y) -> c r v y", v=HALF_COLS, y=2),
+                in_=acc[:].rearrange("c (r y v) -> c r v y", y=2, v=HALF_COLS),
             )
 
         def multiply_and_store(unit):
+            pair, band = divmod(unit, BANDS)
+            band_pixels = slice(band * BAND_PIXELS, (band + 1) * BAND_PIXELS)
             for side in range(SIDES):
-                accs = []
+                image_out = out[pair * SIDES + side].rearrange(
+                    "(half c) h w -> c half (h w)", half=C_HALVES
+                )
+                result = result_pool.tile([P, C_HALVES, BAND_PIXELS], F32)
                 for half in range(C_HALVES):
                     acc = psum.tile([P, BAND_PIXELS], F32)
-                    accs.append(acc)
                     for down in range(TAPS):
                         one_pass(unit, side, half, down, acc)
-                empty_and_store(unit, side, accs)
+                    if unit >= FIRST_SHARED_UNIT and half == 1:
+                        empty(nc.vector.tensor_copy, acc, result[:, half, :])
+                    else:
+                        empty(nc.scalar.copy, acc, result[:, half, :])
+                    if unit == UNITS - 1:
+                        nc.sync.dma_start(
+                            out=image_out[:, half, band_pixels], in_=result[:, half, :]
+                        )
+                if unit < UNITS - 1:
+                    nc.sync.dma_start(out=image_out[:, :, band_pixels], in_=result[:])
 
         def multiply_and_store_first(unit):
             pair, band = divmod(unit, BANDS)
@@ -194,10 +199,7 @@ def tile_customconvmodule_t_kernel(tc, x, weight, bias, grad_out, out):
                     for down in range(TAPS):
                         one_pass(unit, side, half, down, acc)
                     bank_result = result_pool.tile([P, BAND_PIXELS], F32)
-                    nc.scalar.copy(
-                        out=bank_result[:].rearrange("c (r v y) -> c r v y", v=HALF_COLS, y=2),
-                        in_=acc[:].rearrange("c (r y v) -> c r v y", y=2, v=HALF_COLS),
-                    )
+                    empty(nc.scalar.copy, acc, bank_result[:])
                     nc.sync.dma_start(
                         out=out[pair * SIDES + side, half * P : (half + 1) * P].rearrange(
                             "c h w -> c (h w)"
@@ -218,7 +220,6 @@ def tile_customconvmodule_t_kernel(tc, x, weight, bias, grad_out, out):
         group(1, 0)
         copy_weight_to_sides(1)
         group(1, 1)
-        multiply_and_store_first(0)
         for unit in range(1, UNITS):
             if unit + 1 < UNITS:
                 group(unit + 1, 0)
@@ -226,4 +227,6 @@ def tile_customconvmodule_t_kernel(tc, x, weight, bias, grad_out, out):
             if unit + 1 < UNITS:
                 group(unit + 1, 1)
             shift_scales(unit)
+        multiply_and_store_first(0)
+        for unit in range(1, UNITS):
             multiply_and_store(unit)

@@ -20,18 +20,17 @@ SIDES = 2
 SIDE_PARTITIONS = P // SIDES
 IMAGE_PAIRS = IMAGES // SIDES
 C_HALVES = CHANNELS_IN // P
+HALF_WORDS = TAPS * P
 BANDS = 2
 BAND_ROWS = ROWS // BANDS
 BAND_PIXELS = BAND_ROWS * COLS
-BAND_GRAD_ROWS = BAND_ROWS + 1
-BAND_WORDS = BAND_GRAD_ROWS * COLS
 HALF_COLS = COLS // 2
 UNITS = IMAGE_PAIRS * BANDS
-SCALE_PITCH = 576
-BAND_VALUES = BAND_GRAD_ROWS * GRAD_COLS
-FIRST_SHARED_UNIT = 5
-HALF_WORDS = TAPS * P
+UNIT_GRAD_ROWS = (BAND_ROWS + 1, BAND_ROWS)
+UNIT_FIRST_GRAD_ROW = (0, BAND_ROWS + 1)
 PLANE_PITCH = 576
+PAIR_PITCH = 1088
+FIRST_SHARED_UNIT = 5
 
 FLOPS = 2 * IMAGES * ROWS * COLS * TAPS * TAPS * CHANNELS_OUT * CHANNELS_IN
 BYTES = (
@@ -51,19 +50,20 @@ def tile_customconvmodule_t_kernel(tc, x, weight, bias, grad_out, out):
         psum = ctx.enter_context(tc.psum_pool(name="psum", bufs=8))
         ctx.enter_context(tc.manual_schedule())
 
-        grad_codes = keep.tile([P, UNITS, BAND_WORDS], U32, align_bytes=64)
-        grad_scales = keep.tile([P, UNITS, SCALE_PITCH], U8, align_bytes=64)
-        grad_scales_down = keep.tile([P, UNITS, BAND_PIXELS], U8, align_bytes=64)
+        grad_codes = keep.tile([P, IMAGE_PAIRS, PAIR_PITCH], U32, align_bytes=64)
+        grad_scales = keep.tile([P, IMAGE_PAIRS, PAIR_PITCH], U8, align_bytes=64)
+        grad_scales_down = keep.tile([P, IMAGE_PAIRS, ROWS * COLS], U8, align_bytes=64)
         weight_raw = keep.tile([P, CHANNEL_PAIR, CHANNELS_IN, TAPS, TAPS], BF16)
         weight_grouped = keep.tile(
             [P, C_HALVES, TAPS, P, CHANNEL_PAIR, TAPS], BF16, align_bytes=64
         )
-        weight_codes = keep.tile([P, TAPS * CHANNELS_IN], U32, align_bytes=64)
-        weight_scales = keep.tile([P, TAPS * CHANNELS_IN], U8, align_bytes=64)
-        side_codes = keep.tile([P, SIDES, TAPS * CHANNELS_IN], U32, align_bytes=64)
+        weight_codes = keep.tile([P, C_HALVES * HALF_WORDS], U32, align_bytes=64)
+        weight_scales = keep.tile([P, C_HALVES * HALF_WORDS], U8, align_bytes=64)
+        side_codes = keep.tile([P, SIDES, C_HALVES * HALF_WORDS], U32, align_bytes=64)
 
         nc.vector.memset(side_codes[:].bitcast(I32), 0)
         nc.vector.memset(grad_scales[:].bitcast(I32), 0)
+        nc.vector.memset(grad_scales_down[:].bitcast(I32), 0)
 
         weight_rows = weight.rearrange("(q e) c i j -> q (e c i j)", e=CHANNEL_PAIR)
         for side in range(SIDES):
@@ -79,14 +79,15 @@ def tile_customconvmodule_t_kernel(tc, x, weight, bias, grad_out, out):
         for pair in range(IMAGE_PAIRS):
             for band in range(BANDS):
                 raw = raw_pool.tile([P, CHANNEL_PAIR, PLANE_PITCH], BF16, align_bytes=64)
-                first_row = band * BAND_ROWS
+                first_row = UNIT_FIRST_GRAD_ROW[band]
+                values = UNIT_GRAD_ROWS[band] * GRAD_COLS
                 nc.sync.dma_start(
-                    out=raw[:, :, 0:BAND_VALUES],
+                    out=raw[:, :, 0:values],
                     in_=grad_rows[
-                        pair * P : (pair + 1) * P, :, first_row : first_row + BAND_GRAD_ROWS, :
+                        pair * P : (pair + 1) * P, :, first_row : first_row + UNIT_GRAD_ROWS[band], :
                     ].rearrange("p e r s -> p e (r s)"),
                 )
-                raws.append(raw[:, :, 0:BAND_VALUES].rearrange("p e (r s) -> p e r s", s=GRAD_COLS))
+                raws.append(raw[:, :, 0:values].rearrange("p e (r s) -> p e r s", s=GRAD_COLS))
 
         def group_weight(half):
             nc.scalar.copy(
@@ -113,53 +114,79 @@ def tile_customconvmodule_t_kernel(tc, x, weight, bias, grad_out, out):
                     in_=weight_codes[side_rows, half_words].bitcast(I32),
                 )
 
-        groupeds = []
+        groupeds = {}
 
-        def group(unit, parity):
-            if parity == 0:
+        def grouped_of(unit):
+            if unit not in groupeds:
                 grouped = grouped_pool.tile(
-                    [P, BAND_GRAD_ROWS, 2, HALF_COLS, CHANNEL_PAIR, TAPS], BF16, align_bytes=64
+                    [P, BAND_ROWS + 1, 2, HALF_COLS, CHANNEL_PAIR, TAPS], BF16, align_bytes=64
                 )
-                groupeds.append(grouped)
-            for first_row, end_row in ((0, BAND_ROWS), (BAND_ROWS, BAND_GRAD_ROWS)):
-                nc.vector.tensor_copy(
-                    out=groupeds[unit][:, first_row:end_row, parity, :, :, :],
-                    in_=raws[unit][:, :, first_row:end_row, parity : parity + COLS].rearrange(
-                        "q e r (v j) -> q r v e j", j=TAPS
-                    ),
-                )
+                groupeds[unit] = grouped
+            return groupeds[unit]
 
-        def quantise(unit, parts=(0, 1)):
-            values = groupeds[unit][:].rearrange("q r y v e j -> q (r y v e j)")
-            for part in parts:
-                first_word, end_word = ((0, BAND_PIXELS), (BAND_PIXELS, BAND_WORDS))[part]
-                nc.vector.quantize_mx(
-                    out=grad_codes[:, unit, first_word:end_word].bitcast(E5M2_X4),
-                    scales=grad_scales[:, unit, first_word:end_word],
-                    in_=values[:, first_word * PACK : end_word * PACK],
-                )
-
-        def shift_scales(unit):
+        def group(unit, parity, first_row, end_row):
             nc.vector.tensor_copy(
-                out=grad_scales_down[:, unit, :].bitcast(I32),
-                in_=grad_scales[:, unit, COLS:BAND_WORDS].bitcast(I32),
+                out=grouped_of(unit)[:, first_row:end_row, parity, :, :, :],
+                in_=raws[unit][:, :, first_row:end_row, parity : parity + COLS].rearrange(
+                    "q e r (v j) -> q r v e j", j=TAPS
+                ),
             )
 
-        def one_pass(unit, side, half, down, acc):
+        def group_main(unit, parity):
+            group(unit, parity, 0, BAND_ROWS)
+
+        def group_last(unit, parity):
+            if unit % BANDS == 0:
+                group(unit, parity, BAND_ROWS, BAND_ROWS + 1)
+
+        def quantise(unit, first_row, end_row, scales, first_scale):
+            pair, band = divmod(unit, BANDS)
+            values = grouped_of(unit)[:].rearrange("q r y v e j -> q (r y v e j)")
+            first_word = (UNIT_FIRST_GRAD_ROW[band] + first_row) * COLS
+            words = (end_row - first_row) * COLS
+            nc.vector.quantize_mx(
+                out=grad_codes[:, pair, first_word : first_word + words].bitcast(E5M2_X4),
+                scales=scales[:, pair, first_scale : first_scale + words],
+                in_=values[:, first_row * COLS * PACK : end_row * COLS * PACK],
+            )
+
+        def quantise_main(unit):
+            if unit % BANDS == 0:
+                quantise(unit, 0, BAND_ROWS, grad_scales, 0)
+            else:
+                quantise(unit, 0, BAND_ROWS, grad_scales_down, BAND_PIXELS)
+
+        def quantise_last(unit):
+            if unit % BANDS == 0:
+                quantise(unit, BAND_ROWS, BAND_ROWS + 1, grad_scales, BAND_PIXELS)
+
+        def shift_scales(unit):
+            pair, band = divmod(unit, BANDS)
+            if band == 0:
+                nc.vector.tensor_copy(
+                    out=grad_scales_down[:, pair, 0:BAND_PIXELS].bitcast(I32),
+                    in_=grad_scales[:, pair, COLS : COLS + BAND_PIXELS].bitcast(I32),
+                )
+            else:
+                nc.vector.tensor_copy(
+                    out=grad_scales[:, pair, BAND_PIXELS + COLS : ROWS * COLS].bitcast(I32),
+                    in_=grad_scales_down[:, pair, BAND_PIXELS : ROWS * COLS - COLS].bitcast(I32),
+                )
+
+        def one_pass(unit, side, half, down, acc, start, stop):
+            pair, band = divmod(unit, BANDS)
             first_c_word = half * HALF_WORDS + (1 - down) * P
             c_words = slice(first_c_word, first_c_word + P)
+            first_word = band * BAND_PIXELS + down * COLS
+            scales = grad_scales if down == 0 else grad_scales_down
             nc.tensor.matmul_mx(
                 out=acc[:],
                 lhsT=side_codes[:, side, c_words].bitcast(E4M3_X4),
                 lhsT_scale=weight_scales[:, c_words],
-                rhs=grad_codes[:, unit, down * COLS : down * COLS + BAND_PIXELS].bitcast(E5M2_X4),
-                rhs_scale=(
-                    grad_scales[:, unit, 0:BAND_PIXELS]
-                    if down == 0
-                    else grad_scales_down[:, unit, :]
-                ),
-                start=(down == 0),
-                stop=(down == TAPS - 1),
+                rhs=grad_codes[:, pair, first_word : first_word + BAND_PIXELS].bitcast(E5M2_X4),
+                rhs_scale=scales[:, pair, band * BAND_PIXELS : (band + 1) * BAND_PIXELS],
+                start=start,
+                stop=stop,
             )
 
         def empty(copy, acc, target):
@@ -171,19 +198,26 @@ def tile_customconvmodule_t_kernel(tc, x, weight, bias, grad_out, out):
         def multiply_and_store(unit):
             pair, band = divmod(unit, BANDS)
             band_pixels = slice(band * BAND_PIXELS, (band + 1) * BAND_PIXELS)
+            downs = (0, 1) if band == 0 else (1, 0)
             for side in range(SIDES):
                 image_out = out[pair * SIDES + side].rearrange(
                     "(half c) h w -> c half (h w)", half=C_HALVES
                 )
                 result = result_pool.tile([P, C_HALVES, BAND_PIXELS], F32)
+                accs = []
                 for half in range(C_HALVES):
                     acc = psum.tile([P, BAND_PIXELS], F32)
-                    for down in range(TAPS):
-                        one_pass(unit, side, half, down, acc)
+                    accs.append(acc)
+                for down in downs:
+                    for half in range(C_HALVES):
+                        one_pass(
+                            unit, side, half, down, accs[half], down == downs[0], down == downs[1]
+                        )
+                for half in range(C_HALVES):
                     if unit >= FIRST_SHARED_UNIT and half == 1:
-                        empty(nc.vector.tensor_copy, acc, result[:, half, :])
+                        empty(nc.vector.tensor_copy, accs[half], result[:, half, :])
                     else:
-                        empty(nc.scalar.copy, acc, result[:, half, :])
+                        empty(nc.scalar.copy, accs[half], result[:, half, :])
                     if unit == UNITS - 1:
                         nc.sync.dma_start(
                             out=image_out[:, half, band_pixels], in_=result[:, half, :]
@@ -197,7 +231,7 @@ def tile_customconvmodule_t_kernel(tc, x, weight, bias, grad_out, out):
                 for side in range(SIDES):
                     acc = psum.tile([P, BAND_PIXELS], F32)
                     for down in range(TAPS):
-                        one_pass(unit, side, half, down, acc)
+                        one_pass(unit, side, half, down, acc, down == 0, down == TAPS - 1)
                     bank_result = result_pool.tile([P, BAND_PIXELS], F32)
                     empty(nc.scalar.copy, acc, bank_result[:])
                     nc.sync.dma_start(
@@ -209,23 +243,34 @@ def tile_customconvmodule_t_kernel(tc, x, weight, bias, grad_out, out):
 
         group_weight(0)
         group_weight(1)
-        group(0, 0)
-        group(0, 1)
-        quantise(0, (0,))
+        group_main(0, 0)
+        group_main(0, 1)
+        group_last(0, 0)
+        group_last(0, 1)
+        quantise_main(0)
         quantise_weight(0)
-        quantise(0, (1,))
+        quantise_last(0)
         copy_weight_to_sides(0)
         shift_scales(0)
         quantise_weight(1)
-        group(1, 0)
+        group_main(1, 0)
         copy_weight_to_sides(1)
-        group(1, 1)
-        for unit in range(1, UNITS):
+        group_main(1, 1)
+        group_last(2, 0)
+        group_last(2, 1)
+        quantise_main(1)
+        group_main(2, 0)
+        shift_scales(1)
+        group_main(2, 1)
+        for unit in range(2, UNITS):
             if unit + 1 < UNITS:
-                group(unit + 1, 0)
-            quantise(unit)
+                group_main(unit + 1, 0)
+                group_last(unit + 1, 0)
+            quantise_main(unit)
+            quantise_last(unit)
             if unit + 1 < UNITS:
-                group(unit + 1, 1)
+                group_main(unit + 1, 1)
+                group_last(unit + 1, 1)
             shift_scales(unit)
         multiply_and_store_first(0)
         for unit in range(1, UNITS):

@@ -66,11 +66,15 @@ def tile_customconvmodule_t_kernel(tc, x, weight, bias, grad_out, out):
         nc.vector.memset(grad_scales_down[:].bitcast(I32), 0)
 
         weight_rows = weight.rearrange("(q e) c i j -> q (e c i j)", e=CHANNEL_PAIR)
-        for side in range(SIDES):
-            side_rows = slice(side * SIDE_PARTITIONS, (side + 1) * SIDE_PARTITIONS)
-            nc.scalar.dma_start(
-                out=weight_raw[side_rows].rearrange("q e c i j -> q (e c i j)"), in_=weight_rows
-            )
+
+        def load_weight():
+            for side in range(SIDES):
+                side_rows = slice(side * SIDE_PARTITIONS, (side + 1) * SIDE_PARTITIONS)
+                nc.sync.dma_start(
+                    out=weight_raw[side_rows].rearrange("q e c i j -> q (e c i j)"),
+                    in_=weight_rows,
+                )
+
         table_warmer = keep.tile([P, 2], F32)
         nc.gpsimd.memset(table_warmer[:, 0:1], 0.0)
         nc.scalar.copy(out=table_warmer[:, 1:2], in_=table_warmer[:, 0:1])
@@ -88,6 +92,8 @@ def tile_customconvmodule_t_kernel(tc, x, weight, bias, grad_out, out):
                     ].rearrange("p e r s -> p e (r s)"),
                 )
                 raws.append(raw[:, :, 0:values].rearrange("p e (r s) -> p e r s", s=GRAD_COLS))
+                if pair == 0 and band == 0:
+                    load_weight()
 
         def group_weight(half):
             nc.scalar.copy(

@@ -95,8 +95,8 @@ def tile_customconvmodule_t_kernel(tc, x, weight, bias, grad_out, out):
                 if pair == 0 and band == 0:
                     load_weight()
 
-        def group_weight(half):
-            nc.scalar.copy(
+        def group_weight(copy, half):
+            copy(
                 out=weight_grouped[:, half, :, :, :, :],
                 in_=weight_raw[:, :, half * P : (half + 1) * P, :, ::-1].rearrange(
                     "q e c i j -> q i c e j"
@@ -247,17 +247,17 @@ def tile_customconvmodule_t_kernel(tc, x, weight, bias, grad_out, out):
                         in_=bank_result[:],
                     )
 
-        group_weight(0)
-        group_weight(1)
+        group_weight(nc.scalar.copy, 1)
         group_main(0, 0)
         group_main(0, 1)
         group_last(0, 0)
         group_last(0, 1)
         quantise_main(0)
-        quantise_weight(0)
+        group_weight(nc.vector.tensor_copy, 0)
         quantise_last(0)
-        copy_weight_to_sides(0)
+        quantise_weight(0)
         shift_scales(0)
+        copy_weight_to_sides(0)
         quantise_weight(1)
         group_main(1, 0)
         copy_weight_to_sides(1)

@@ -28,6 +28,7 @@ HALF_COLS = COLS // 2
 UNITS = IMAGE_PAIRS * BANDS
 UNIT_GRAD_ROWS = (BAND_ROWS + 1, BAND_ROWS)
 UNIT_FIRST_GRAD_ROW = (0, BAND_ROWS + 1)
+WARM_MATMULS = 8
 PLANE_PITCH = 576
 PAIR_PITCH = 1088
 FIRST_SHARED_UNIT = 5
@@ -64,6 +65,14 @@ def tile_customconvmodule_t_kernel(tc, x, weight, bias, grad_out, out):
         nc.vector.memset(side_codes[:].bitcast(I32), 0)
         nc.vector.memset(grad_scales[:].bitcast(I32), 0)
         nc.vector.memset(grad_scales_down[:].bitcast(I32), 0)
+
+        warm_values = keep.tile([P, BAND_PIXELS], BF16)
+        nc.vector.memset(warm_values[:].bitcast(I32), 0)
+        acc = psum.tile([P, BAND_PIXELS], F32)
+        for matmul in range(WARM_MATMULS):
+            nc.tensor.matmul(
+                out=acc[:], lhsT=warm_values[:, 0:P], rhs=warm_values[:], start=True, stop=True
+            )
 
         weight_rows = weight.rearrange("(q e) c i j -> q (e c i j)", e=CHANNEL_PAIR)
 
@@ -130,16 +139,16 @@ def tile_customconvmodule_t_kernel(tc, x, weight, bias, grad_out, out):
                 groupeds[unit] = grouped
             return groupeds[unit]
 
-        def group(unit, parity, first_row, end_row):
-            nc.vector.tensor_copy(
+        def group(unit, parity, first_row, end_row, copy=nc.vector.tensor_copy):
+            copy(
                 out=grouped_of(unit)[:, first_row:end_row, parity, :, :, :],
                 in_=raws[unit][:, :, first_row:end_row, parity : parity + COLS].rearrange(
                     "q e r (v j) -> q r v e j", j=TAPS
                 ),
             )
 
-        def group_main(unit, parity):
-            group(unit, parity, 0, BAND_ROWS)
+        def group_main(unit, parity, copy=nc.vector.tensor_copy):
+            group(unit, parity, 0, BAND_ROWS, copy)
 
         def group_last(unit, parity):
             if unit % BANDS == 0:
@@ -248,6 +257,7 @@ def tile_customconvmodule_t_kernel(tc, x, weight, bias, grad_out, out):
                     )
 
         group_weight(nc.scalar.copy, 1)
+        group_main(1, 1, nc.scalar.copy)
         group_main(0, 0)
         group_main(0, 1)
         group_last(0, 0)
@@ -261,22 +271,20 @@ def tile_customconvmodule_t_kernel(tc, x, weight, bias, grad_out, out):
         quantise_weight(1)
         group_main(1, 0)
         copy_weight_to_sides(1)
-        group_main(1, 1)
-        group_last(2, 0)
-        group_last(2, 1)
         quantise_main(1)
-        group_main(2, 0)
+        group_last(2, 0)
         shift_scales(1)
-        group_main(2, 1)
+        group_main(2, 0)
         for unit in range(2, UNITS):
-            if unit + 1 < UNITS:
-                group_main(unit + 1, 0)
+            group_main(unit, 1)
+            if unit % BANDS == 0:
+                group_last(unit, 1)
+            elif unit + 1 < UNITS:
                 group_last(unit + 1, 0)
             quantise_main(unit)
             quantise_last(unit)
             if unit + 1 < UNITS:
-                group_main(unit + 1, 1)
-                group_last(unit + 1, 1)
+                group_main(unit + 1, 0)
             shift_scales(unit)
         multiply_and_store_first(0)
         for unit in range(1, UNITS):

@@ -28,7 +28,8 @@ HALF_COLS = COLS // 2
 UNITS = IMAGE_PAIRS * BANDS
 UNIT_GRAD_ROWS = (BAND_ROWS + 1, BAND_ROWS)
 UNIT_FIRST_GRAD_ROW = (0, BAND_ROWS + 1)
-WARM_MATMULS = 8
+WARM_MATMULS = 5
+SCALAR_FIRST_ROW = 12
 PLANE_PITCH = 576
 PAIR_PITCH = 1088
 FIRST_SHARED_UNIT = 5
@@ -64,15 +65,7 @@ def tile_customconvmodule_t_kernel(tc, x, weight, bias, grad_out, out):
 
         nc.vector.memset(side_codes[:].bitcast(I32), 0)
         nc.vector.memset(grad_scales[:].bitcast(I32), 0)
-        nc.vector.memset(grad_scales_down[:].bitcast(I32), 0)
-
-        warm_values = keep.tile([P, BAND_PIXELS], BF16)
-        nc.vector.memset(warm_values[:].bitcast(I32), 0)
-        acc = psum.tile([P, BAND_PIXELS], F32)
-        for matmul in range(WARM_MATMULS):
-            nc.tensor.matmul(
-                out=acc[:], lhsT=warm_values[:, 0:P], rhs=warm_values[:], start=True, stop=True
-            )
+        nc.gpsimd.memset(grad_scales_down[:].bitcast(I32), 0)
 
         weight_rows = weight.rearrange("(q e) c i j -> q (e c i j)", e=CHANNEL_PAIR)
 
@@ -89,6 +82,7 @@ def tile_customconvmodule_t_kernel(tc, x, weight, bias, grad_out, out):
         nc.scalar.copy(out=table_warmer[:, 1:2], in_=table_warmer[:, 0:1])
         grad_rows = grad_out.rearrange("b (q e) r s -> (b q) e r s", e=CHANNEL_PAIR)
         raws = []
+        raw_tiles = []
         for pair in range(IMAGE_PAIRS):
             for band in range(BANDS):
                 raw = raw_pool.tile([P, CHANNEL_PAIR, PLANE_PITCH], BF16, align_bytes=64)
@@ -100,9 +94,20 @@ def tile_customconvmodule_t_kernel(tc, x, weight, bias, grad_out, out):
                         pair * P : (pair + 1) * P, :, first_row : first_row + UNIT_GRAD_ROWS[band], :
                     ].rearrange("p e r s -> p e (r s)"),
                 )
+                raw_tiles.append(raw)
                 raws.append(raw[:, :, 0:values].rearrange("p e (r s) -> p e r s", s=GRAD_COLS))
                 if pair == 0 and band == 0:
                     load_weight()
+
+        acc = psum.tile([P, BAND_PIXELS], F32)
+        for matmul in range(WARM_MATMULS):
+            nc.tensor.matmul(
+                out=acc[:],
+                lhsT=raw_tiles[0][:, 0, 0:P],
+                rhs=raw_tiles[0][:, 1, 0:BAND_PIXELS],
+                start=True,
+                stop=True,
+            )
 
         def group_weight(copy, half):
             copy(
@@ -256,12 +261,12 @@ def tile_customconvmodule_t_kernel(tc, x, weight, bias, grad_out, out):
                         in_=bank_result[:],
                     )
 
+        group(0, 1, SCALAR_FIRST_ROW, BAND_ROWS + 1, nc.scalar.copy)
         group_weight(nc.scalar.copy, 1)
         group_main(1, 1, nc.scalar.copy)
         group_main(0, 0)
-        group_main(0, 1)
+        group(0, 1, 0, SCALAR_FIRST_ROW)
         group_last(0, 0)
-        group_last(0, 1)
         quantise_main(0)
         group_weight(nc.vector.tensor_copy, 0)
         quantise_last(0)

@@ -67,14 +67,15 @@ def tile_customconvmodule_t_kernel(tc, x, weight, bias, grad_out, out):
         nc.vector.memset(grad_scales[:].bitcast(I32), 0)
         nc.gpsimd.memset(grad_scales_down[:].bitcast(I32), 0)
 
-        weight_rows = weight.rearrange("(q e) c i j -> q (e c i j)", e=CHANNEL_PAIR)
+        weight_rows = weight.rearrange("(q e) c i j -> q e c i j", e=CHANNEL_PAIR)
 
-        def load_weight():
+        def load_weight(half):
+            c_rows = slice(half * P, (half + 1) * P)
             for side in range(SIDES):
                 side_rows = slice(side * SIDE_PARTITIONS, (side + 1) * SIDE_PARTITIONS)
                 nc.sync.dma_start(
-                    out=weight_raw[side_rows].rearrange("q e c i j -> q (e c i j)"),
-                    in_=weight_rows,
+                    out=weight_raw[side_rows, :, c_rows, :, :].rearrange("q e c i j -> q e (c i j)"),
+                    in_=weight_rows[:, :, c_rows, :, :].rearrange("q e c i j -> q e (c i j)"),
                 )
 
         table_warmer = keep.tile([P, 2], F32)
@@ -97,7 +98,8 @@ def tile_customconvmodule_t_kernel(tc, x, weight, bias, grad_out, out):
                 raw_tiles.append(raw)
                 raws.append(raw[:, :, 0:values].rearrange("p e (r s) -> p e r s", s=GRAD_COLS))
                 if pair == 0 and band == 0:
-                    load_weight()
+                    for half in range(C_HALVES):
+                        load_weight(half)
 
         acc = psum.tile([P, BAND_PIXELS], F32)
         for matmul in range(WARM_MATMULS):
@@ -263,7 +265,7 @@ def tile_customconvmodule_t_kernel(tc, x, weight, bias, grad_out, out):
 
         group(0, 1, SCALAR_FIRST_ROW, BAND_ROWS + 1, nc.scalar.copy)
         group_weight(nc.scalar.copy, 1)
-        group_main(1, 1, nc.scalar.copy)
+        group(1, 1, BAND_ROWS // 2, BAND_ROWS, nc.scalar.copy)
         group_main(0, 0)
         group(0, 1, 0, SCALAR_FIRST_ROW)
         group_last(0, 0)
@@ -274,6 +276,7 @@ def tile_customconvmodule_t_kernel(tc, x, weight, bias, grad_out, out):
         shift_scales(0)
         copy_weight_to_sides(0)
         quantise_weight(1)
+        group(1, 1, 0, BAND_ROWS // 2)
         group_main(1, 0)
         copy_weight_to_sides(1)
         quantise_main(1)

from contextlib import ExitStack

import concourse.mybir as mybir

BF16 = mybir.dt.bfloat16
F32 = mybir.dt.float32
I32 = mybir.dt.int32
U32 = mybir.dt.uint32
U8 = mybir.dt.uint8
E4M3_X4 = mybir.dt.float8_e4m3fn_x4
E5M2_X4 = mybir.dt.float8_e5m2_x4

P = 128
IMAGES, CHANNELS_OUT, GRAD_ROWS, GRAD_COLS = 8, 128, 33, 33
CHANNELS_IN, ROWS, COLS = 256, 32, 32
PACK = 4
CHANNEL_PAIR = 2
TAPS = 2
SIDES = 2
SIDE_PARTITIONS = P // SIDES
IMAGE_PAIRS = IMAGES // SIDES
C_HALVES = CHANNELS_IN // P
HALF_WORDS = TAPS * P
BANDS = 2
BAND_ROWS = ROWS // BANDS
BAND_PIXELS = BAND_ROWS * COLS
HALF_COLS = COLS // 2
UNITS = IMAGE_PAIRS * BANDS
UNIT_GRAD_ROWS = (BAND_ROWS + 1, BAND_ROWS)
UNIT_FIRST_GRAD_ROW = (0, BAND_ROWS + 1)
WARM_MATMULS = 5
SCALAR_FIRST_ROW = 12
PLANE_PITCH = 576
PAIR_PITCH = 1088
FIRST_SHARED_UNIT = 5

FLOPS = 2 * IMAGES * ROWS * COLS * TAPS * TAPS * CHANNELS_OUT * CHANNELS_IN
BYTES = (
    2 * CHANNELS_OUT * CHANNELS_IN * TAPS * TAPS
    + 2 * IMAGES * CHANNELS_OUT * GRAD_ROWS * GRAD_COLS
    + 4 * IMAGES * CHANNELS_IN * ROWS * COLS
)


def tile_customconvmodule_t_kernel(tc, x, weight, bias, grad_out, out):
    nc = tc.nc
    with ExitStack() as ctx:
        keep = ctx.enter_context(tc.tile_pool(name="keep", bufs=1))
        raw_pool = ctx.enter_context(tc.tile_pool(name="raw", bufs=UNITS))
        grouped_pool = ctx.enter_context(tc.tile_pool(name="grouped", bufs=3))
        result_pool = ctx.enter_context(tc.tile_pool(name="result", bufs=8))
        psum = ctx.enter_context(tc.psum_pool(name="psum", bufs=8))
        ctx.enter_context(tc.manual_schedule())

        grad_codes = keep.tile([P, IMAGE_PAIRS, PAIR_PITCH], U32, align_bytes=64)
        grad_scales = keep.tile([P, IMAGE_PAIRS, PAIR_PITCH], U8, align_bytes=64)
        grad_scales_down = keep.tile([P, IMAGE_PAIRS, ROWS * COLS], U8, align_bytes=64)
        weight_raw = keep.tile([P, CHANNEL_PAIR, CHANNELS_IN, TAPS, TAPS], BF16)
        weight_grouped = keep.tile(
            [P, C_HALVES, TAPS, P, CHANNEL_PAIR, TAPS], BF16, align_bytes=64
        )
        weight_codes = keep.tile([P, C_HALVES * HALF_WORDS], U32, align_bytes=64)
        weight_scales = keep.tile([P, C_HALVES * HALF_WORDS], U8, align_bytes=64)
        side_codes = keep.tile([P, SIDES, C_HALVES * HALF_WORDS], U32, align_bytes=64)

        nc.vector.memset(side_codes[:].bitcast(I32), 0)
        nc.vector.memset(grad_scales[:].bitcast(I32), 0)
        nc.gpsimd.memset(grad_scales_down[:].bitcast(I32), 0)

        weight_rows = weight.rearrange("(q e) c i j -> q e c i j", e=CHANNEL_PAIR)

        def load_weight(half):
            c_rows = slice(half * P, (half + 1) * P)
            for side in range(SIDES):
                side_rows = slice(side * SIDE_PARTITIONS, (side + 1) * SIDE_PARTITIONS)
                nc.sync.dma_start(
                    out=weight_raw[side_rows, :, c_rows, :, :].rearrange("q e c i j -> q e (c i j)"),
                    in_=weight_rows[:, :, c_rows, :, :].rearrange("q e c i j -> q e (c i j)"),
                )

        table_warmer = keep.tile([P, 2], F32)
        nc.gpsimd.memset(table_warmer[:, 0:1], 0.0)
        nc.scalar.copy(out=table_warmer[:, 1:2], in_=table_warmer[:, 0:1])
        grad_rows = grad_out.rearrange("b (q e) r s -> (b q) e r s", e=CHANNEL_PAIR)
        raws = []
        raw_tiles = []
        for pair in range(IMAGE_PAIRS):
            for band in range(BANDS):
                raw = raw_pool.tile([P, CHANNEL_PAIR, PLANE_PITCH], BF16, align_bytes=64)
                first_row = UNIT_FIRST_GRAD_ROW[band]
                values = UNIT_GRAD_ROWS[band] * GRAD_COLS
                nc.sync.dma_start(
                    out=raw[:, :, 0:values],
                    in_=grad_rows[
                        pair * P : (pair + 1) * P, :, first_row : first_row + UNIT_GRAD_ROWS[band], :
                    ].rearrange("p e r s -> p e (r s)"),
                )
                raw_tiles.append(raw)
                raws.append(raw[:, :, 0:values].rearrange("p e (r s) -> p e r s", s=GRAD_COLS))
                if pair == 0 and band == 0:
                    for half in range(C_HALVES):
                        load_weight(half)

        acc = psum.tile([P, BAND_PIXELS], F32)
        for matmul in range(WARM_MATMULS):
            nc.tensor.matmul(
                out=acc[:],
                lhsT=raw_tiles[0][:, 0, 0:P],
                rhs=raw_tiles[0][:, 1, 0:BAND_PIXELS],
                start=True,
                stop=True,
            )

        def group_weight(copy, half):
            copy(
                out=weight_grouped[:, half, :, :, :, :],
                in_=weight_raw[:, :, half * P : (half + 1) * P, :, ::-1].rearrange(
                    "q e c i j -> q i c e j"
                ),
            )

        def quantise_weight(half):
            half_words = slice(half * HALF_WORDS, (half + 1) * HALF_WORDS)
            nc.vector.quantize_mx(
                out=weight_codes[:, half_words].bitcast(E4M3_X4),
                scales=weight_scales[:, half_words],
                in_=weight_grouped[:, half, :, :, :, :].rearrange("q i c e j -> q (i c e j)"),
            )

        def copy_weight_to_sides(half):
            half_words = slice(half * HALF_WORDS, (half + 1) * HALF_WORDS)
            for side in range(SIDES):
                side_rows = slice(side * SIDE_PARTITIONS, (side + 1) * SIDE_PARTITIONS)
                nc.vector.tensor_copy(
                    out=side_codes[side_rows, side, half_words].bitcast(I32),
                    in_=weight_codes[side_rows, half_words].bitcast(I32),
                )

        groupeds = {}

        def grouped_of(unit):
            if unit not in groupeds:
                grouped = grouped_pool.tile(
                    [P, BAND_ROWS + 1, 2, HALF_COLS, CHANNEL_PAIR, TAPS], BF16, align_bytes=64
                )
                groupeds[unit] = grouped
            return groupeds[unit]

        def group(unit, parity, first_row, end_row, copy=nc.vector.tensor_copy):
            copy(
                out=grouped_of(unit)[:, first_row:end_row, parity, :, :, :],
                in_=raws[unit][:, :, first_row:end_row, parity : parity + COLS].rearrange(
                    "q e r (v j) -> q r v e j", j=TAPS
                ),
            )

        def group_main(unit, parity, copy=nc.vector.tensor_copy):
            group(unit, parity, 0, BAND_ROWS, copy)

        def group_last(unit, parity):
            if unit % BANDS == 0:
                group(unit, parity, BAND_ROWS, BAND_ROWS + 1)

        def quantise(unit, first_row, end_row, scales, first_scale):
            pair, band = divmod(unit, BANDS)
            values = grouped_of(unit)[:].rearrange("q r y v e j -> q (r y v e j)")
            first_word = (UNIT_FIRST_GRAD_ROW[band] + first_row) * COLS
            words = (end_row - first_row) * COLS
            nc.vector.quantize_mx(
                out=grad_codes[:, pair, first_word : first_word + words].bitcast(E5M2_X4),
                scales=scales[:, pair, first_scale : first_scale + words],
                in_=values[:, first_row * COLS * PACK : end_row * COLS * PACK],
            )

        def quantise_main(unit):
            if unit % BANDS == 0:
                quantise(unit, 0, BAND_ROWS, grad_scales, 0)
            else:
                quantise(unit, 0, BAND_ROWS, grad_scales_down, BAND_PIXELS)

        def quantise_last(unit):
            if unit % BANDS == 0:
                quantise(unit, BAND_ROWS, BAND_ROWS + 1, grad_scales, BAND_PIXELS)

        def shift_scales(unit):
            pair, band = divmod(unit, BANDS)
            if band == 0:
                nc.vector.tensor_copy(
                    out=grad_scales_down[:, pair, 0:BAND_PIXELS].bitcast(I32),
                    in_=grad_scales[:, pair, COLS : COLS + BAND_PIXELS].bitcast(I32),
                )
            else:
                nc.vector.tensor_copy(
                    out=grad_scales[:, pair, BAND_PIXELS + COLS : ROWS * COLS].bitcast(I32),
                    in_=grad_scales_down[:, pair, BAND_PIXELS : ROWS * COLS - COLS].bitcast(I32),
                )

        def one_pass(unit, side, half, down, acc, start, stop):
            pair, band = divmod(unit, BANDS)
            first_c_word = half * HALF_WORDS + (1 - down) * P
            c_words = slice(first_c_word, first_c_word + P)
            first_word = band * BAND_PIXELS + down * COLS
            scales = grad_scales if down == 0 else grad_scales_down
            nc.tensor.matmul_mx(
                out=acc[:],
                lhsT=side_codes[:, side, c_words].bitcast(E4M3_X4),
                lhsT_scale=weight_scales[:, c_words],
                rhs=grad_codes[:, pair, first_word : first_word + BAND_PIXELS].bitcast(E5M2_X4),
                rhs_scale=scales[:, pair, band * BAND_PIXELS : (band + 1) * BAND_PIXELS],
                start=start,
                stop=stop,
            )

        def empty(copy, acc, target):
            copy(
                out=target.rearrange("c (r v y) -> c r v y", v=HALF_COLS, y=2),
                in_=acc[:].rearrange("c (r y v) -> c r v y", y=2, v=HALF_COLS),
            )

        def multiply_and_store(unit):
            pair, band = divmod(unit, BANDS)
            band_pixels = slice(band * BAND_PIXELS, (band + 1) * BAND_PIXELS)
            downs = (0, 1) if band == 0 else (1, 0)
            for side in range(SIDES):
                image_out = out[pair * SIDES + side].rearrange(
                    "(half c) h w -> c half (h w)", half=C_HALVES
                )
                result = result_pool.tile([P, C_HALVES, BAND_PIXELS], F32)
                accs = []
                for half in range(C_HALVES):
                    acc = psum.tile([P, BAND_PIXELS], F32)
                    accs.append(acc)
                for down in downs:
                    for half in range(C_HALVES):
                        one_pass(
                            unit, side, half, down, accs[half], down == downs[0], down == downs[1]
                        )
                for half in range(C_HALVES):
                    if unit >= FIRST_SHARED_UNIT and half == 1:
                        empty(nc.vector.tensor_copy, accs[half], result[:, half, :])
                    else:
                        empty(nc.scalar.copy, accs[half], result[:, half, :])
                    if unit == UNITS - 1:
                        nc.sync.dma_start(
                            out=image_out[:, half, band_pixels], in_=result[:, half, :]
                        )
                if unit < UNITS - 1:
                    nc.sync.dma_start(out=image_out[:, :, band_pixels], in_=result[:])

        def multiply_and_store_first(unit):
            pair, band = divmod(unit, BANDS)
            for half in range(C_HALVES):
                for side in range(SIDES):
                    acc = psum.tile([P, BAND_PIXELS], F32)
                    for down in range(TAPS):
                        one_pass(unit, side, half, down, acc, down == 0, down == TAPS - 1)
                    bank_result = result_pool.tile([P, BAND_PIXELS], F32)
                    empty(nc.scalar.copy, acc, bank_result[:])
                    nc.sync.dma_start(
                        out=out[pair * SIDES + side, half * P : (half + 1) * P].rearrange(
                            "c h w -> c (h w)"
                        )[:, band * BAND_PIXELS : (band + 1) * BAND_PIXELS],
                        in_=bank_result[:],
                    )

        group(0, 1, SCALAR_FIRST_ROW, BAND_ROWS + 1, nc.scalar.copy)
        group_weight(nc.scalar.copy, 1)
        group(1, 1, BAND_ROWS // 2, BAND_ROWS, nc.scalar.copy)
        group_main(0, 0)
        group(0, 1, 0, SCALAR_FIRST_ROW)
        group_last(0, 0)
        quantise_main(0)
        group_weight(nc.vector.tensor_copy, 0)
        quantise_last(0)
        quantise_weight(0)
        shift_scales(0)
        copy_weight_to_sides(0)
        quantise_weight(1)
        group(1, 1, 0, BAND_ROWS // 2)
        group_main(1, 0)
        copy_weight_to_sides(1)
        quantise_main(1)
        group_last(2, 0)
        shift_scales(1)
        group_main(2, 0)
        for unit in range(2, UNITS):
            group_main(unit, 1)
            if unit % BANDS == 0:
                group_last(unit, 1)
            elif unit + 1 < UNITS:
                group_last(unit + 1, 0)
            quantise_main(unit)
            quantise_last(unit)
            if unit + 1 < UNITS:
                group_main(unit + 1, 0)
            shift_scales(unit)
        multiply_and_store_first(0)
        for unit in range(1, UNITS):
            multiply_and_store(unit)
